import numpy as np
import ml_dtypes


def mxq(x, axis, fmt="e4m3"):
    dtype, down = {"e4m3": (ml_dtypes.float8_e4m3fn, 7), "e5m2": (ml_dtypes.float8_e5m2, 14)}[fmt]
    v = np.moveaxis(np.asarray(x, np.float32).astype(ml_dtypes.bfloat16).astype(np.float64), axis, -1)
    blocks = v.reshape(v.shape[:-1] + (-1, 32))
    amax = np.abs(blocks).max(-1, keepdims=True)
    byte = np.maximum(np.where(amax > 0, np.frexp(amax)[1] - 1 + 127, 0) - down, 1)
    scale = np.exp2(byte - 127.0)
    codes = (blocks / scale).astype(np.float32).astype(dtype).astype(np.float64)
    return np.moveaxis((codes * scale).reshape(v.shape), -1, axis)


WIDE = False


def mx_kscale(k):
    if not WIDE:
        return np.ones(k)
    levels = np.array([10, -10, 5, -5, 0])
    a = np.random.permutation(np.resize(levels, k // 512 * 4)).reshape(k // 512, 4)
    idx = np.arange(k)
    return np.exp2(a[idx // 512, idx % 128 // 32])


BF16 = ml_dtypes.bfloat16


def bf(x):
    return np.asarray(x, np.float32).astype(BF16)


def f64(x):
    return np.asarray(x).astype(np.float64)


NB, S, D, O, E, R = 4, 128, 2048, 2048, 32, 16
ER = E * R
SCALING = 2.0


def softmax(v):
    e = np.exp(v - v.max(-1, keepdims=True))
    return e / e.sum(-1, keepdims=True)


def setup_inputs():
    s, t = mx_kscale(D), mx_kscale(ER)
    return {
        "x": bf(np.random.standard_normal((NB, S, D)) * s),
        "gate_logits": bf(np.random.standard_normal((NB, S, E)) * 1.5),
        "W_base": bf(np.random.standard_normal((O, D)) / np.sqrt(D) / s),
        "b_base": bf(np.random.standard_normal(O) * 0.3),
        "A": bf(np.random.standard_normal((E, R, D)) / np.sqrt(D) / s * t.reshape(E, R, 1)),
        "B": bf(np.random.standard_normal((E, O, R)) / np.sqrt(R) / t.reshape(E, 1, R)),
    }


def reference(x, gate_logits, W_base, b_base, A, B):
    xq = mxq(f64(x), 2, "e4m3")
    result = (xq @ mxq(f64(W_base), 1, "e4m3").T) + f64(b_base)
    route = softmax(f64(gate_logits))
    h = (xq @ mxq(f64(A).reshape(ER, D), 1, "e4m3").T).reshape(NB, S, E, R)
    hw = (h * route[..., None]).reshape(NB, S, ER)
    b_flat = f64(B).transpose(0, 2, 1).reshape(ER, O)
    return result + SCALING * (mxq(hw, 2, "e4m3") @ mxq(b_flat, 0, "e4m3"))

@@ -1,0 +1,308 @@
+from contextlib import ExitStack
+
+import concourse.mybir as mybir
+from concourse.masks import make_identity
+
+F32 = mybir.dt.float32
+BF16 = mybir.dt.bfloat16
+U32 = mybir.dt.uint32
+U8 = mybir.dt.uint8
+FP8X4 = mybir.dt.float8_e4m3fn_x4
+ALU = mybir.AluOpType
+ACT = mybir.ActivationFunctionType
+AX = mybir.AxisListType
+
+P = 128
+TT = 4
+D = 2048
+O = 2048
+E = 32
+R = 16
+NG = 4
+NC = 4
+FLOPS = 2 * 512 * D * O + 2 * 512 * D * 512 + 2 * 512 * 512 * O
+
+
+def tile_linearmoloralayer_pa_kernel(tc, x, gate_logits, W_base, b_base, A, B, out):
+    nc = tc.nc
+    xf = x.flatten_outer_dims()
+    gf = gate_logits.flatten_outer_dims()
+    af = A.flatten_outer_dims().rearrange("(u p e) d -> u e p d", u=2, e=2)
+    of = out.flatten_outer_dims()
+
+    with ExitStack() as ctx:
+        const = ctx.enter_context(tc.tile_pool(name="const", bufs=1))
+        grpp = ctx.enter_context(tc.tile_pool(name="grpp", bufs=3))
+        bsp = ctx.enter_context(tc.tile_pool(name="bsp", bufs=2))
+        wcp = ctx.enter_context(tc.tile_pool(name="wcp", bufs=3))
+        outp = ctx.enter_context(tc.tile_pool(name="outp", bufs=4))
+        accp = ctx.enter_context(tc.psum_pool(name="accp", bufs=1))
+        stp = ctx.enter_context(tc.psum_pool(name="stp", bufs=4))
+        ctx.enter_context(tc.manual_schedule())
+
+        ident = const.tile([P, P], F32)
+        make_identity(nc, ident[:])
+        ones = const.tile([P, P], BF16)
+        nc.gpsimd.memset(ones[:], 1.0)
+        brow = const.tile([P, O], BF16)
+        nc.vector.memset(brow[:], 0.0)
+
+        gl = const.tile([P, TT, E], BF16)
+        nc.sync.dma_start(out=gl[:], in_=gf.rearrange("(t p) e -> p t e", p=P))
+        xr = []
+        for t in range(TT):
+            r = const.tile([P, D], BF16, name="xr%d" % t)
+            nc.sync.dma_start(out=r[:], in_=xf[t * P:(t + 1) * P, :])
+            xr.append(r)
+        nc.sync.dma_start(out=brow[0:1, :], in_=b_base.rearrange("(o n) -> o n", o=1))
+        ar = []
+        for t in range(4):
+            r = const.tile([P, D], BF16, name="ar%d" % t)
+            nc.sync.dma_start(out=r[:], in_=af[t // 2, t % 2, :, :])
+            ar.append(r)
+        wr = []
+        bsb = const.tile([P, E, 256], BF16)
+        for j in range(16):
+            r = const.tile([P, D], BF16, name="wr%d" % j)
+            nc.sync.dma_start(out=r[:], in_=W_base[j * P:(j + 1) * P, :])
+            wr.append(r)
+            if j == 3:
+                nc.sync.dma_start(out=bsb[:], in_=B.rearrange("e (p s) r -> p e (s r)", s=16))
+
+        xc = const.tile([P, TT, 512], U32, align_bytes=64)
+        xs = const.tile([P, TT, 512], U8, align_bytes=64)
+        ac = const.tile([P, 4, 512], U32, align_bytes=64)
+        asc = const.tile([P, 4, 512], U8, align_bytes=64)
+        bc = const.tile([P, O], U32, align_bytes=64)
+        bsc = const.tile([P, O], U8, align_bytes=64)
+        hc = const.tile([P, 512], U32, align_bytes=64)
+        hsc = const.tile([P, 512], U8, align_bytes=64)
+        hwg = const.tile([P, 2048], BF16, align_bytes=64)
+        bg = const.tile([P, 4 * O], BF16, align_bytes=64)
+        bias_bc = const.tile([P, O], F32)
+        rt = const.tile([P, TT, 2, P], F32)
+
+        mx = const.tile([P, TT], F32)
+        nc.vector.tensor_reduce(out=mx[:], in_=gl[:], axis=AX.X, op=ALU.max)
+        dl = const.tile([P, TT, E], F32)
+        nc.vector.tensor_tensor(out=dl[:], in0=gl[:], in1=mx[:].unsqueeze(2).to_broadcast([P, TT, E]), op=ALU.subtract)
+        ex = const.tile([P, TT, E], F32)
+        nc.scalar.activation(out=ex[:], in_=dl[:], func=ACT.Exp)
+        sm = const.tile([P, TT], F32)
+        nc.vector.tensor_reduce(out=sm[:], in_=ex[:], axis=AX.X, op=ALU.add)
+        rc = const.tile([P, TT], F32)
+        nc.vector.reciprocal(out=rc[:], in_=sm[:])
+        rc2 = const.tile([P, TT], F32)
+        nc.vector.tensor_scalar_mul(out=rc2[:], in0=rc[:], scalar1=2.0)
+        rexp = const.tile([P, TT, E, 8], F32)
+        nc.vector.tensor_tensor(
+            out=rexp[:],
+            in0=ex[:].unsqueeze(3).to_broadcast([P, TT, E, 8]),
+            in1=rc2[:].unsqueeze(2).unsqueeze(3).to_broadcast([P, TT, E, 8]),
+            op=ALU.mult,
+        )
+
+        grps = {}
+        wcs = {}
+        accs = {}
+
+        def flip(i, views):
+            grp = grpp.tile([P, 2048], BF16, tag="grp", align_bytes=64)
+            grps[i] = grp
+            words = grp[:].bitcast(F32)
+            for b in range(2):
+                st = stp.tile([P, 512], F32, tag="st")
+                for s in range(4):
+                    nc.tensor.transpose(st[:, s * P:(s + 1) * P], views[4 * b + s], ident[:])
+                nc.scalar.copy(
+                    out=words[:, 512 * b:512 * (b + 1)].rearrange("p (j n u) -> p j n u", j=2, u=2),
+                    in_=st[:].rearrange("p (j u n) -> p j n u", j=2, u=2),
+                )
+
+        def row_views(r):
+            w = r[:].bitcast(F32)
+            return [w[:, c * P:(c + 1) * P] for c in range(8)]
+
+        def w_views(c, g):
+            res = []
+            for j in range(4):
+                w = wr[4 * c + j][:].bitcast(F32)
+                for u in range(2):
+                    res.append(w[:, 256 * g + P * u:256 * g + P * u + P])
+            return res
+
+        def quant_to(i, codes, scales):
+            nc.vector.quantize_mx(out=codes.bitcast(FP8X4), scales=scales, in_=grps[i][:])
+
+        def quant_w(i):
+            wc = wcp.tile([P, 512], U32, tag="wc", align_bytes=64)
+            ws = wcp.tile([P, 512], U8, tag="ws", align_bytes=64)
+            wcs[i] = (wc, ws)
+            nc.vector.quantize_mx(out=wc[:].bitcast(FP8X4), scales=ws[:], in_=grps[i][:])
+
+        def new_acc(key):
+            tiles = []
+            for tt in range(TT):
+                a = accp.tile([P, 512], F32, tag="acc%d" % tt, name="acc%d" % tt)
+                tiles.append(a)
+            accs[key] = tiles
+            return tiles
+
+        def bias_job():
+            tiles = new_acc("bias")
+            for c in range(NC):
+                nc.tensor.matmul(out=tiles[c][:], lhsT=ones[:], rhs=brow[:, c * 512:(c + 1) * 512], start=True, stop=True)
+                nc.vector.tensor_copy(out=bias_bc[:, c * 512:(c + 1) * 512], in_=tiles[c][:])
+
+        def route_job():
+            rw = rexp[:].rearrange("p t e i -> p t (e i)")
+            for b in range(2):
+                st = stp.tile([P, 512], F32, tag="st")
+                for s in range(4):
+                    nc.tensor.transpose(st[:, s * P:(s + 1) * P], rw[:, 2 * b + s // 2, (s % 2) * P:(s % 2 + 1) * P], ident[:])
+                nc.scalar.copy(out=rt[:, 2 * b:2 * b + 2, :, :].rearrange("p t u n -> p (t u n)"), in_=st[:])
+
+        def h_job(t):
+            if t == 0:
+                new_acc("h")
+            hps = accs["h"]
+            for tt in range(TT):
+                for g in range(NG):
+                    nc.tensor.matmul_mx(
+                        out=hps[tt][:, t * P:(t + 1) * P],
+                        lhsT=ac[:, t, g * P:(g + 1) * P].bitcast(FP8X4),
+                        lhsT_scale=asc[:, t, g * P:(g + 1) * P],
+                        rhs=xc[:, tt, g * P:(g + 1) * P].bitcast(FP8X4),
+                        rhs_scale=xs[:, tt, g * P:(g + 1) * P],
+                        start=(g == 0),
+                        stop=(g == NG - 1),
+                    )
+            if t == 3:
+                for tt in range(TT):
+                    nc.vector.tensor_tensor(
+                        out=hwg[:, tt * 512:(tt + 1) * 512].rearrange("p (n u e) -> p n u e", u=2, e=2),
+                        in0=hps[tt][:].rearrange("p (u e n) -> p n u e", u=2, e=2),
+                        in1=rt[:, tt, :, :].rearrange("p u n -> p n u").unsqueeze(3).to_broadcast([P, P, 2, 2]),
+                        op=ALU.mult,
+                    )
+                nc.vector.quantize_mx(out=hc[:].bitcast(FP8X4), scales=hsc[:], in_=hwg[:])
+
+        def b_job(q):
+            bs = bsp.tile([P, 2048], BF16, tag="bs")
+            nc.vector.tensor_copy(
+                out=bs[:].rearrange("p (s e r) -> p s e r", s=4, r=R),
+                in_=bsb[:].rearrange("p e (s r) -> p s e r", r=R)[:, 4 * q:4 * q + 4, :, :],
+            )
+            bw = bs[:].bitcast(F32)
+            bgw = bg[:].bitcast(F32).rearrange("p (n s u) -> p n s u", s=16, u=2)
+            for b in range(2):
+                st = stp.tile([P, 512], F32, tag="st")
+                for s in range(4):
+                    col = (2 * b + s // 2) * 256 + (s % 2) * P
+                    nc.tensor.transpose(st[:, s * P:(s + 1) * P], bw[:, col:col + P], ident[:])
+                os0 = 4 * q + 2 * b
+                nc.scalar.copy(
+                    out=bgw[:, :, os0:os0 + 2, :],
+                    in_=st[:].rearrange("p (s u n) -> p n s u", s=2, u=2),
+                )
+
+        def quant_b():
+            for h in range(2):
+                nc.vector.quantize_mx(
+                    out=bc[:, h * 1024:(h + 1) * 1024].bitcast(FP8X4),
+                    scales=bsc[:, h * 1024:(h + 1) * 1024],
+                    in_=bg[:, h * 4096:(h + 1) * 4096],
+                )
+
+        def lora_job(c, start, stop):
+            acc = accs[c]
+            for tt in range(TT):
+                nc.tensor.matmul_mx(
+                    out=acc[tt][:],
+                    lhsT=hc[:, tt * P:(tt + 1) * P].bitcast(FP8X4),
+                    lhsT_scale=hsc[:, tt * P:(tt + 1) * P],
+                    rhs=bc[:, c * 512:(c + 1) * 512].bitcast(FP8X4),
+                    rhs_scale=bsc[:, c * 512:(c + 1) * 512],
+                    start=start,
+                    stop=stop,
+                )
+
+        def base_job(i, c, g, start, stop):
+            acc = accs[c]
+            wc, ws = wcs[i]
+            for tt in range(TT):
+                nc.tensor.matmul_mx(
+                    out=acc[tt][:],
+                    lhsT=xc[:, tt, g * P:(g + 1) * P].bitcast(FP8X4),
+                    lhsT_scale=xs[:, tt, g * P:(g + 1) * P],
+                    rhs=wc[:].bitcast(FP8X4),
+                    rhs_scale=ws[:],
+                    start=start,
+                    stop=stop,
+                )
+
+        def evac(c):
+            acc = accs[c]
+            for tt in range(TT):
+                osb = outp.tile([P, 512], F32, tag="osb")
+                nc.vector.tensor_tensor(out=osb[:], in0=acc[tt][:], in1=bias_bc[:, c * 512:(c + 1) * 512], op=ALU.add)
+                nc.sync.dma_start(out=of[tt * P:(tt + 1) * P, c * 512:(c + 1) * 512], in_=osb[:])
+
+        tj = []
+        qj = []
+        pj = []
+
+        def add(t, q, p):
+            tj.append(t)
+            qj.append(q)
+            pj.append(p)
+
+        for t in range(TT):
+            i = len(tj)
+            add(
+                lambda i=i, t=t: flip(i, row_views(xr[t])),
+                lambda i=i, t=t: quant_to(i, xc[:, t, :], xs[:, t, :]),
+                bias_job if t == 1 else None,
+            )
+        add(route_job, None, None)
+        for t in range(4):
+            i = len(tj)
+            add(
+                lambda i=i, t=t: flip(i, row_views(ar[t])),
+                lambda i=i, t=t: quant_to(i, ac[:, t, :], asc[:, t, :]),
+                lambda t=t: h_job(t),
+            )
+
+        def p_w(i, c, g):
+            if g == 0:
+                new_acc(c)
+                if c > 0:
+                    lora_job(c, True, False)
+            base_job(i, c, g, (c == 0 and g == 0), (c > 0 and g == NG - 1))
+            if c > 0 and g == NG - 1:
+                evac(c)
+
+        def p_b_last():
+            lora_job(0, False, True)
+            evac(0)
+
+        for c in range(NC):
+            for g in range(NG):
+                i = len(tj)
+                add(
+                    lambda i=i, c=c, g=g: flip(i, w_views(c, g)),
+                    lambda i=i: quant_w(i),
+                    lambda i=i, c=c, g=g: p_w(i, c, g),
+                )
+            if c == 0:
+                for q in range(4):
+                    add(lambda q=q: b_job(q), quant_b if q == 3 else None, p_b_last if q == 3 else None)
+
+        n = len(tj)
+        for s in range(-2, n):
+            if s + 2 < n and tj[s + 2] is not None:
+                tj[s + 2]()
+            if 0 <= s + 1 < n and qj[s + 1] is not None:
+                qj[s + 1]()
+            if s >= 0 and pj[s] is not None:
+                pj[s]()

@@ -21,6 +21,7 @@ R = 16
 NG = 4
 NC = 4
 FLOPS = 2 * 512 * D * O + 2 * 512 * D * 512 + 2 * 512 * 512 * O
+DEFERRED = (0,)
 
 
 def tile_linearmoloralayer_pa_kernel(tc, x, gate_logits, W_base, b_base, A, B, out):
@@ -32,8 +33,9 @@ def tile_linearmoloralayer_pa_kernel(tc, x, gate_logits, W_base, b_base, A, B, o
 
     with ExitStack() as ctx:
         const = ctx.enter_context(tc.tile_pool(name="const", bufs=1))
+        rawp = ctx.enter_context(tc.tile_pool(name="rawp", bufs=8))
         grpp = ctx.enter_context(tc.tile_pool(name="grpp", bufs=3))
-        bsp = ctx.enter_context(tc.tile_pool(name="bsp", bufs=2))
+        bsp = ctx.enter_context(tc.tile_pool(name="bsp", bufs=4))
         wcp = ctx.enter_context(tc.tile_pool(name="wcp", bufs=3))
         outp = ctx.enter_context(tc.tile_pool(name="outp", bufs=4))
         accp = ctx.enter_context(tc.psum_pool(name="accp", bufs=1))
@@ -42,32 +44,44 @@ def tile_linearmoloralayer_pa_kernel(tc, x, gate_logits, W_base, b_base, A, B, o
 
         ident = const.tile([P, P], F32)
         make_identity(nc, ident[:])
-        ones = const.tile([P, P], BF16)
-        nc.gpsimd.memset(ones[:], 1.0)
-        brow = const.tile([P, O], BF16)
-        nc.vector.memset(brow[:], 0.0)
+        warm = const.tile([P, 1], F32)
+        nc.vector.memset(warm[:], 0.0)
+        nc.scalar.activation(out=warm[:], in_=warm[:], func=ACT.Exp)
 
+        raws = {}
         gl = const.tile([P, TT, E], BF16)
-        nc.sync.dma_start(out=gl[:], in_=gf.rearrange("(t p) e -> p t e", p=P))
-        xr = []
         for t in range(TT):
-            r = const.tile([P, D], BF16, name="xr%d" % t)
-            nc.sync.dma_start(out=r[:], in_=xf[t * P:(t + 1) * P, :])
-            xr.append(r)
-        nc.sync.dma_start(out=brow[0:1, :], in_=b_base.rearrange("(o n) -> o n", o=1))
-        ar = []
-        for t in range(4):
-            r = const.tile([P, D], BF16, name="ar%d" % t)
-            nc.sync.dma_start(out=r[:], in_=af[t // 2, t % 2, :, :])
-            ar.append(r)
-        wr = []
-        bsb = const.tile([P, E, 256], BF16)
-        for j in range(16):
-            r = const.tile([P, D], BF16, name="wr%d" % j)
-            nc.sync.dma_start(out=r[:], in_=W_base[j * P:(j + 1) * P, :])
-            wr.append(r)
-            if j == 3:
-                nc.sync.dma_start(out=bsb[:], in_=B.rearrange("e (p s) r -> p e (s r)", s=16))
+            r = rawp.tile([P, 4096], BF16, tag="raw")
+            nc.sync.dma_start(out=r[:, D:2 * D], in_=af[t // 2, t % 2, :, :])
+            nc.sync.dma_start(out=r[:, 0:D], in_=xf[t * P:(t + 1) * P, :])
+            raws[("xa", t)] = r
+            if t == 0:
+                nc.sync.dma_start(out=gl[:], in_=gf.rearrange("(t p) e -> p t e", p=P))
+        bview = B.rearrange("e (p s) r -> p e (s r)", s=16)
+
+        def load_w(c, d):
+            r = rawp.tile([P, 4096], BF16, tag="raw")
+            nc.sync.dma_start(
+                out=r[:].rearrange("p (j k) -> p j k", j=4),
+                in_=W_base[c * 512:(c + 1) * 512, d * 1024:(d + 1) * 1024].rearrange("(j p) k -> p j k", p=P),
+            )
+            raws[("w", c, d)] = r
+
+        bias_bc = const.tile([P, O], BF16)
+
+        def load_bias():
+            nc.sync.dma_start(out=bias_bc[:], in_=b_base.partition_broadcast(P))
+
+        def load_b(h):
+            r = rawp.tile([P, 4096], BF16, tag="raw")
+            nc.sync.dma_start(out=r[:].rearrange("p (e k) -> p e k", e=16), in_=bview[:, 16 * h:16 * h + 16, :])
+            raws[("b", h)] = r
+
+        load_w(0, 0)
+        load_w(0, 1)
+        load_bias()
+        load_w(1, 0)
+        load_b(0)
 
         xc = const.tile([P, TT, 512], U32, align_bytes=64)
         xs = const.tile([P, TT, 512], U8, align_bytes=64)
@@ -79,66 +93,82 @@ def tile_linearmoloralayer_pa_kernel(tc, x, gate_logits, W_base, b_base, A, B, o
         hsc = const.tile([P, 512], U8, align_bytes=64)
         hwg = const.tile([P, 2048], BF16, align_bytes=64)
         bg = const.tile([P, 4 * O], BF16, align_bytes=64)
-        bias_bc = const.tile([P, O], F32)
         rt = const.tile([P, TT, 2, P], F32)
+        keep = const.tile([P, len(DEFERRED) * TT, 512], F32)
 
-        mx = const.tile([P, TT], F32)
-        nc.vector.tensor_reduce(out=mx[:], in_=gl[:], axis=AX.X, op=ALU.max)
-        dl = const.tile([P, TT, E], F32)
-        nc.vector.tensor_tensor(out=dl[:], in0=gl[:], in1=mx[:].unsqueeze(2).to_broadcast([P, TT, E]), op=ALU.subtract)
+        rexp = bsp.tile([P, TT, E, 8], F32, tag="bs")
+
         ex = const.tile([P, TT, E], F32)
-        nc.scalar.activation(out=ex[:], in_=dl[:], func=ACT.Exp)
-        sm = const.tile([P, TT], F32)
-        nc.vector.tensor_reduce(out=sm[:], in_=ex[:], axis=AX.X, op=ALU.add)
-        rc = const.tile([P, TT], F32)
-        nc.vector.reciprocal(out=rc[:], in_=sm[:])
-        rc2 = const.tile([P, TT], F32)
-        nc.vector.tensor_scalar_mul(out=rc2[:], in0=rc[:], scalar1=2.0)
-        rexp = const.tile([P, TT, E, 8], F32)
-        nc.vector.tensor_tensor(
-            out=rexp[:],
-            in0=ex[:].unsqueeze(3).to_broadcast([P, TT, E, 8]),
-            in1=rc2[:].unsqueeze(2).unsqueeze(3).to_broadcast([P, TT, E, 8]),
-            op=ALU.mult,
-        )
+
+        def softmax_head():
+            mx = const.tile([P, TT], F32)
+            nc.vector.tensor_reduce(out=mx[:], in_=gl[:], axis=AX.X, op=ALU.max)
+            dl = const.tile([P, TT, E], F32)
+            nc.vector.tensor_tensor(out=dl[:], in0=gl[:], in1=mx[:].unsqueeze(2).to_broadcast([P, TT, E]), op=ALU.subtract)
+            nc.scalar.activation(out=ex[:], in_=dl[:], func=ACT.Exp)
+
+        def softmax_tail():
+            sm = const.tile([P, TT], F32)
+            nc.vector.tensor_reduce(out=sm[:], in_=ex[:], axis=AX.X, op=ALU.add)
+            rc = const.tile([P, TT], F32)
+            nc.vector.reciprocal(out=rc[:], in_=sm[:])
+            rc2 = const.tile([P, TT], F32)
+            nc.vector.tensor_scalar_mul(out=rc2[:], in0=rc[:], scalar1=2.0)
+            nc.vector.tensor_tensor(
+                out=rexp[:],
+                in0=ex[:].unsqueeze(3).to_broadcast([P, TT, E, 8]),
+                in1=rc2[:].unsqueeze(2).unsqueeze(3).to_broadcast([P, TT, E, 8]),
+                op=ALU.mult,
+            )
 
         grps = {}
         wcs = {}
         accs = {}
 
-        def flip(i, views):
+        def flip_bank(views, words, eng):
+            st = stp.tile([P, 512], F32, tag="st")
+            for s in range(4):
+                nc.tensor.transpose(st[:, s * P:(s + 1) * P], views[s], ident[:])
+            src = st[:].rearrange("p (j u n) -> p j n u", j=2, u=2)
+            dst = words.rearrange("p (j n u) -> p j n u", j=2, u=2)
+            if eng == "v":
+                nc.vector.tensor_copy(out=dst, in_=src)
+            else:
+                nc.scalar.copy(out=dst, in_=src)
+
+        def t_xa(kind, t):
             grp = grpp.tile([P, 2048], BF16, tag="grp", align_bytes=64)
-            grps[i] = grp
+            grps[(kind, t)] = grp
+            w = raws[("xa", t)][:].bitcast(F32)
+            base = 0 if kind == "x" else 1024
             words = grp[:].bitcast(F32)
             for b in range(2):
-                st = stp.tile([P, 512], F32, tag="st")
-                for s in range(4):
-                    nc.tensor.transpose(st[:, s * P:(s + 1) * P], views[4 * b + s], ident[:])
-                nc.scalar.copy(
-                    out=words[:, 512 * b:512 * (b + 1)].rearrange("p (j n u) -> p j n u", j=2, u=2),
-                    in_=st[:].rearrange("p (j u n) -> p j n u", j=2, u=2),
+                flip_bank([w[:, base + (4 * b + s) * P:base + (4 * b + s + 1) * P] for s in range(4)], words[:, 512 * b:512 * (b + 1)], "s")
+
+        def q_xa(kind, t):
+            codes, scales = (xc, xs) if kind == "x" else (ac, asc)
+            nc.vector.quantize_mx(out=codes[:, t, :].bitcast(FP8X4), scales=scales[:, t, :], in_=grps[(kind, t)][:])
+
+        def t_w(c, d, engs="ssss"):
+            grp = grpp.tile([P, 4096], BF16, tag="grp", align_bytes=64)
+            grps[("w", c, d)] = grp
+            w = raws[("w", c, d)][:].bitcast(F32)
+            words = grp[:].bitcast(F32)
+            for k in range(2):
+                for b in range(2):
+                    views = [w[:, (2 * b + s // 2) * 512 + k * 256 + (s % 2) * P:(2 * b + s // 2) * 512 + k * 256 + (s % 2) * P + P] for s in range(4)]
+                    flip_bank(views, words[:, 1024 * k + 512 * b:1024 * k + 512 * (b + 1)], engs[2 * k + b])
+
+        def q_w(c, d):
+            wc = wcp.tile([P, 1024], U32, tag="wc", align_bytes=64)
+            ws = wcp.tile([P, 1024], U8, tag="ws", align_bytes=64)
+            wcs[(c, d)] = (wc, ws)
+            for k in range(2):
+                nc.vector.quantize_mx(
+                    out=wc[:, k * 512:(k + 1) * 512].bitcast(FP8X4),
+                    scales=ws[:, k * 512:(k + 1) * 512],
+                    in_=grps[("w", c, d)][:, k * 2048:(k + 1) * 2048],
                 )
-
-        def row_views(r):
-            w = r[:].bitcast(F32)
-            return [w[:, c * P:(c + 1) * P] for c in range(8)]
-
-        def w_views(c, g):
-            res = []
-            for j in range(4):
-                w = wr[4 * c + j][:].bitcast(F32)
-                for u in range(2):
-                    res.append(w[:, 256 * g + P * u:256 * g + P * u + P])
-            return res
-
-        def quant_to(i, codes, scales):
-            nc.vector.quantize_mx(out=codes.bitcast(FP8X4), scales=scales, in_=grps[i][:])
-
-        def quant_w(i):
-            wc = wcp.tile([P, 512], U32, tag="wc", align_bytes=64)
-            ws = wcp.tile([P, 512], U8, tag="ws", align_bytes=64)
-            wcs[i] = (wc, ws)
-            nc.vector.quantize_mx(out=wc[:].bitcast(FP8X4), scales=ws[:], in_=grps[i][:])
 
         def new_acc(key):
             tiles = []
@@ -148,12 +178,6 @@ def tile_linearmoloralayer_pa_kernel(tc, x, gate_logits, W_base, b_base, A, B, o
             accs[key] = tiles
             return tiles
 
-        def bias_job():
-            tiles = new_acc("bias")
-            for c in range(NC):
-                nc.tensor.matmul(out=tiles[c][:], lhsT=ones[:], rhs=brow[:, c * 512:(c + 1) * 512], start=True, stop=True)
-                nc.vector.tensor_copy(out=bias_bc[:, c * 512:(c + 1) * 512], in_=tiles[c][:])
-
         def route_job():
             rw = rexp[:].rearrange("p t e i -> p t (e i)")
             for b in range(2):
@@ -162,147 +186,202 @@ def tile_linearmoloralayer_pa_kernel(tc, x, gate_logits, W_base, b_base, A, B, o
                     nc.tensor.transpose(st[:, s * P:(s + 1) * P], rw[:, 2 * b + s // 2, (s % 2) * P:(s % 2 + 1) * P], ident[:])
                 nc.scalar.copy(out=rt[:, 2 * b:2 * b + 2, :, :].rearrange("p t u n -> p (t u n)"), in_=st[:])
 
-        def h_job(t):
-            if t == 0:
-                new_acc("h")
+        def h_group(t, tt):
             hps = accs["h"]
-            for tt in range(TT):
-                for g in range(NG):
-                    nc.tensor.matmul_mx(
-                        out=hps[tt][:, t * P:(t + 1) * P],
-                        lhsT=ac[:, t, g * P:(g + 1) * P].bitcast(FP8X4),
-                        lhsT_scale=asc[:, t, g * P:(g + 1) * P],
-                        rhs=xc[:, tt, g * P:(g + 1) * P].bitcast(FP8X4),
-                        rhs_scale=xs[:, tt, g * P:(g + 1) * P],
-                        start=(g == 0),
-                        stop=(g == NG - 1),
-                    )
-            if t == 3:
-                for tt in range(TT):
-                    nc.vector.tensor_tensor(
-                        out=hwg[:, tt * 512:(tt + 1) * 512].rearrange("p (n u e) -> p n u e", u=2, e=2),
-                        in0=hps[tt][:].rearrange("p (u e n) -> p n u e", u=2, e=2),
-                        in1=rt[:, tt, :, :].rearrange("p u n -> p n u").unsqueeze(3).to_broadcast([P, P, 2, 2]),
-                        op=ALU.mult,
-                    )
-                nc.vector.quantize_mx(out=hc[:].bitcast(FP8X4), scales=hsc[:], in_=hwg[:])
-
-        def b_job(q):
-            bs = bsp.tile([P, 2048], BF16, tag="bs")
-            nc.vector.tensor_copy(
-                out=bs[:].rearrange("p (s e r) -> p s e r", s=4, r=R),
-                in_=bsb[:].rearrange("p e (s r) -> p s e r", r=R)[:, 4 * q:4 * q + 4, :, :],
-            )
-            bw = bs[:].bitcast(F32)
-            bgw = bg[:].bitcast(F32).rearrange("p (n s u) -> p n s u", s=16, u=2)
-            for b in range(2):
-                st = stp.tile([P, 512], F32, tag="st")
-                for s in range(4):
-                    col = (2 * b + s // 2) * 256 + (s % 2) * P
-                    nc.tensor.transpose(st[:, s * P:(s + 1) * P], bw[:, col:col + P], ident[:])
-                os0 = 4 * q + 2 * b
-                nc.scalar.copy(
-                    out=bgw[:, :, os0:os0 + 2, :],
-                    in_=st[:].rearrange("p (s u n) -> p n s u", s=2, u=2),
+            for g in range(NG):
+                nc.tensor.matmul_mx(
+                    out=hps[tt][:, t * P:(t + 1) * P],
+                    lhsT=ac[:, t, g * P:(g + 1) * P].bitcast(FP8X4),
+                    lhsT_scale=asc[:, t, g * P:(g + 1) * P],
+                    rhs=xc[:, tt, g * P:(g + 1) * P].bitcast(FP8X4),
+                    rhs_scale=xs[:, tt, g * P:(g + 1) * P],
+                    start=(g == 0),
+                    stop=(g == NG - 1),
                 )
 
-        def quant_b():
+        def hw_mult(tt):
+            nc.vector.tensor_tensor(
+                out=hwg[:, tt * 512:(tt + 1) * 512].rearrange("p (n u e) -> p n u e", u=2, e=2),
+                in0=accs["h"][tt][:].rearrange("p (u e n) -> p n u e", u=2, e=2),
+                in1=rt[:, tt, :, :].rearrange("p u n -> p n u").unsqueeze(3).to_broadcast([P, P, 2, 2]),
+                op=ALU.mult,
+            )
+
+        def hw_quant():
+            nc.vector.quantize_mx(out=hc[:].bitcast(FP8X4), scales=hsc[:], in_=hwg[:])
+
+        def shuffle_b(q):
+            bs = bsp.tile([P, 2048], BF16, tag="bs")
+            grps[("bs", q)] = bs
             for h in range(2):
+                nc.vector.tensor_copy(
+                    out=bs[:].rearrange("p (s e r) -> p s e r", s=4, r=R)[:, :, 16 * h:16 * h + 16, :],
+                    in_=raws[("b", h)][:].rearrange("p (e s r) -> p s e r", e=16, r=R)[:, 4 * q:4 * q + 4, :, :],
+                )
+
+        def t_b(half, engs):
+            bgw = bg[:].bitcast(F32).rearrange("p (n s u) -> p n s u", s=16, u=2)
+            for q in (2 * half, 2 * half + 1):
+                bw = grps[("bs", q)][:].bitcast(F32)
+                for b in range(2):
+                    st = stp.tile([P, 512], F32, tag="st")
+                    for s in range(4):
+                        col = (2 * b + s // 2) * 256 + (s % 2) * P
+                        nc.tensor.transpose(st[:, s * P:(s + 1) * P], bw[:, col:col + P], ident[:])
+                    os0 = 4 * q + 2 * b
+                    src = st[:].rearrange("p (s u n) -> p n s u", s=2, u=2)
+                    if engs[q % 2] == "v":
+                        nc.vector.tensor_copy(out=bgw[:, :, os0:os0 + 2, :], in_=src)
+                    else:
+                        nc.scalar.copy(out=bgw[:, :, os0:os0 + 2, :], in_=src)
+
+        def q_b(hs):
+            for h in hs:
                 nc.vector.quantize_mx(
                     out=bc[:, h * 1024:(h + 1) * 1024].bitcast(FP8X4),
                     scales=bsc[:, h * 1024:(h + 1) * 1024],
                     in_=bg[:, h * 4096:(h + 1) * 4096],
                 )
 
-        def lora_job(c, start, stop):
-            acc = accs[c]
-            for tt in range(TT):
-                nc.tensor.matmul_mx(
-                    out=acc[tt][:],
-                    lhsT=hc[:, tt * P:(tt + 1) * P].bitcast(FP8X4),
-                    lhsT_scale=hsc[:, tt * P:(tt + 1) * P],
-                    rhs=bc[:, c * 512:(c + 1) * 512].bitcast(FP8X4),
-                    rhs_scale=bsc[:, c * 512:(c + 1) * 512],
-                    start=start,
-                    stop=stop,
-                )
-
-        def base_job(i, c, g, start, stop):
-            acc = accs[c]
-            wc, ws = wcs[i]
-            for tt in range(TT):
-                nc.tensor.matmul_mx(
-                    out=acc[tt][:],
-                    lhsT=xc[:, tt, g * P:(g + 1) * P].bitcast(FP8X4),
-                    lhsT_scale=xs[:, tt, g * P:(g + 1) * P],
-                    rhs=wc[:].bitcast(FP8X4),
-                    rhs_scale=ws[:],
-                    start=start,
-                    stop=stop,
-                )
-
-        def evac(c):
-            acc = accs[c]
-            for tt in range(TT):
-                osb = outp.tile([P, 512], F32, tag="osb")
-                nc.vector.tensor_tensor(out=osb[:], in0=acc[tt][:], in1=bias_bc[:, c * 512:(c + 1) * 512], op=ALU.add)
-                nc.sync.dma_start(out=of[tt * P:(tt + 1) * P, c * 512:(c + 1) * 512], in_=osb[:])
-
-        tj = []
-        qj = []
-        pj = []
-
-        def add(t, q, p):
-            tj.append(t)
-            qj.append(q)
-            pj.append(p)
-
-        for t in range(TT):
-            i = len(tj)
-            add(
-                lambda i=i, t=t: flip(i, row_views(xr[t])),
-                lambda i=i, t=t: quant_to(i, xc[:, t, :], xs[:, t, :]),
-                bias_job if t == 1 else None,
-            )
-        add(route_job, None, None)
-        for t in range(4):
-            i = len(tj)
-            add(
-                lambda i=i, t=t: flip(i, row_views(ar[t])),
-                lambda i=i, t=t: quant_to(i, ac[:, t, :], asc[:, t, :]),
-                lambda t=t: h_job(t),
+        def lora_pass(dst, c, tt, start, stop):
+            nc.tensor.matmul_mx(
+                out=dst[:],
+                lhsT=hc[:, tt * P:(tt + 1) * P].bitcast(FP8X4),
+                lhsT_scale=hsc[:, tt * P:(tt + 1) * P],
+                rhs=bc[:, c * 512:(c + 1) * 512].bitcast(FP8X4),
+                rhs_scale=bsc[:, c * 512:(c + 1) * 512],
+                start=start,
+                stop=stop,
             )
 
-        def p_w(i, c, g):
+        def base_pass(c, g, tt, start, stop):
+            wc, ws = wcs[(c, g // 2)]
+            k = g % 2
+            nc.tensor.matmul_mx(
+                out=accs[c][tt][:],
+                lhsT=xc[:, tt, g * P:(g + 1) * P].bitcast(FP8X4),
+                lhsT_scale=xs[:, tt, g * P:(g + 1) * P],
+                rhs=wc[:, k * 512:(k + 1) * 512].bitcast(FP8X4),
+                rhs_scale=ws[:, k * 512:(k + 1) * 512],
+                start=start,
+                stop=stop,
+            )
+
+        def store(c, tt, src):
+            nc.sync.dma_start(out=of[tt * P:(tt + 1) * P, c * 512:(c + 1) * 512], in_=src)
+
+        def p4(c, g):
             if g == 0:
                 new_acc(c)
-                if c > 0:
-                    lora_job(c, True, False)
-            base_job(i, c, g, (c == 0 and g == 0), (c > 0 and g == NG - 1))
-            if c > 0 and g == NG - 1:
-                evac(c)
+            for tt in range(TT):
+                base_pass(c, g, tt, g == 0, False)
 
-        def p_b_last():
-            lora_job(0, False, True)
-            evac(0)
+        def evac(c, tt):
+            if c in DEFERRED:
+                dst = keep[:, DEFERRED.index(c) * TT + tt, :]
+            else:
+                osb = outp.tile([P, 512], F32, tag="osb")
+                dst = osb[:]
+            nc.vector.tensor_tensor(out=dst, in0=accs[c][tt][:], in1=bias_bc[:, c * 512:(c + 1) * 512], op=ALU.add)
+            if c not in DEFERRED:
+                store(c, tt, dst)
 
-        for c in range(NC):
-            for g in range(NG):
-                i = len(tj)
-                add(
-                    lambda i=i, c=c, g=g: flip(i, w_views(c, g)),
-                    lambda i=i: quant_w(i),
-                    lambda i=i, c=c, g=g: p_w(i, c, g),
-                )
-            if c == 0:
-                for q in range(4):
-                    add(lambda q=q: b_job(q), quant_b if q == 3 else None, p_b_last if q == 3 else None)
+        def p_close(c, gs, tts):
+            late = c in DEFERRED
+            for tt in tts:
+                for g in gs:
+                    base_pass(c, g, tt, False, late and g == NG - 1)
+                if not late:
+                    lora_pass(accs[c][tt], c, tt, False, True)
+                evac(c, tt)
 
-        n = len(tj)
-        for s in range(-2, n):
-            if s + 2 < n and tj[s + 2] is not None:
-                tj[s + 2]()
-            if 0 <= s + 1 < n and qj[s + 1] is not None:
-                qj[s + 1]()
-            if s >= 0 and pj[s] is not None:
-                pj[s]()
+        def late_lora(c, where):
+            banks = []
+            for tt in range(TT):
+                if where == "acc":
+                    a = accp.tile([P, 512], F32, tag="acc%d" % tt, name="late%d" % tt)
+                else:
+                    a = stp.tile([P, 512], F32, tag="st", name="late")
+                banks.append(a)
+                lora_pass(a, c, tt, True, True)
+            for tt in range(TT):
+                osb = outp.tile([P, 512], F32, tag="osb")
+                nc.vector.tensor_tensor(out=osb[:], in0=banks[tt][:], in1=keep[:, DEFERRED.index(c) * TT + tt, :], op=ALU.add)
+                store(c, tt, osb[:])
+
+        arr = []
+        for t in range(TT):
+            arr.append(("a", t))
+            arr.append(("x", t))
+        done = []
+        new_acc("h")
+        for k in range(len(arr) + 2):
+            if k < len(arr):
+                t_xa(arr[k][0], arr[k][1])
+            if k == 2:
+                softmax_head()
+            if k == 4:
+                softmax_tail()
+            if k == 5:
+                route_job()
+            if k == 8:
+                load_w(1, 1)
+                load_b(1)
+                load_w(2, 0)
+                load_w(2, 1)
+                t_w(0, 0)
+            if 1 <= k <= len(arr):
+                q_xa(arr[k - 1][0], arr[k - 1][1])
+            if k == 9:
+                q_w(0, 0)
+                t_w(0, 1)
+            if 2 <= k:
+                done.append(arr[k - 2])
+                for t2 in range(TT):
+                    for t1 in range(4):
+                        if ("a", t1) in done and ("x", t2) in done and (t1, t2) not in done:
+                            done.append((t1, t2))
+                            h_group(t1, t2)
+                            if t1 == 3:
+                                hw_mult(t2)
+
+        hw_quant()
+        p4(0, 0)
+        p4(0, 1)
+        q_w(0, 1)
+        t_w(1, 0)
+        load_w(3, 0)
+        p_close(0, (2, 3), (0, 1))
+        q_w(1, 0)
+        p_close(0, (2, 3), (2, 3))
+        t_w(1, 1)
+        load_w(3, 1)
+        for q in range(2):
+            shuffle_b(q)
+        p4(1, 0)
+        q_w(1, 1)
+        t_b(0, "ss")
+        for q in range(2, 4):
+            shuffle_b(q)
+        p4(1, 1)
+        t_b(1, "sv")
+        p4(1, 2)
+        t_w(2, 0)
+        q_b((0,))
+        p4(1, 3)
+        q_w(2, 0)
+        p_close(1, (), (0, 1, 2, 3))
+        t_w(2, 1)
+        late_lora(0, "acc")
+        q_w(2, 1)
+        t_w(3, 0)
+        q_b((1,))
+        p4(2, 0)
+        p4(2, 1)
+        q_w(3, 0)
+        t_w(3, 1)
+        p_close(2, (2, 3), (0, 1, 2, 3))
+        q_w(3, 1)
+        p4(3, 0)
+        p4(3, 1)
+        p_close(3, (2, 3), (0, 1, 2, 3))

@@ -44,12 +44,19 @@ def tile_linearmoloralayer_pa_kernel(tc, x, gate_logits, W_base, b_base, A, B, o
 
         ident = const.tile([P, P], F32)
         make_identity(nc, ident[:])
+        ones = const.tile([P, P], BF16)
+        nc.vector.memset(ones[:], 1.0)
+        zeros = const.tile([P, 512], BF16)
+        nc.vector.memset(zeros[:], 0.0)
+        brow = bsp.tile([P, O], BF16, tag="bs")
+        nc.vector.memset(brow[:], 0.0)
         warm = const.tile([P, 1], F32)
         nc.vector.memset(warm[:], 0.0)
         nc.scalar.activation(out=warm[:], in_=warm[:], func=ACT.Exp)
 
         raws = {}
         gl = const.tile([P, TT, E], BF16)
+        nc.sync.dma_start(out=brow[0:1, :], in_=b_base.rearrange("(o n) -> o n", o=1))
         for t in range(TT):
             r = rawp.tile([P, 4096], BF16, tag="raw")
             nc.sync.dma_start(out=r[:, D:2 * D], in_=af[t // 2, t % 2, :, :])
@@ -67,10 +74,7 @@ def tile_linearmoloralayer_pa_kernel(tc, x, gate_logits, W_base, b_base, A, B, o
             )
             raws[("w", c, d)] = r
 
-        bias_bc = const.tile([P, O], BF16)
-
-        def load_bias():
-            nc.sync.dma_start(out=bias_bc[:], in_=b_base.partition_broadcast(P))
+        bias_bc = const.tile([P, O], F32)
 
         def load_b(h):
             r = rawp.tile([P, 4096], BF16, tag="raw")
@@ -79,7 +83,6 @@ def tile_linearmoloralayer_pa_kernel(tc, x, gate_logits, W_base, b_base, A, B, o
 
         load_w(0, 0)
         load_w(0, 1)
-        load_bias()
         load_w(1, 0)
         load_b(0)
 
@@ -125,8 +128,27 @@ def tile_linearmoloralayer_pa_kernel(tc, x, gate_logits, W_base, b_base, A, B, o
         wcs = {}
         accs = {}
 
-        def flip_bank(views, words, eng):
+        def dummy(st):
+            nc.tensor.matmul(out=st[:], lhsT=ones[:], rhs=zeros[:], start=True, stop=True)
+
+        def warm_up(n):
             st = stp.tile([P, 512], F32, tag="st")
+            for i in range(n):
+                dummy(st)
+
+        def bias_job():
+            for c in range(NC):
+                st = stp.tile([P, 512], F32, tag="st")
+                nc.tensor.matmul(out=st[:], lhsT=ones[:], rhs=brow[:, c * 512:(c + 1) * 512], start=True, stop=True)
+                if c % 2 == 0:
+                    nc.vector.tensor_copy(out=bias_bc[:, c * 512:(c + 1) * 512], in_=st[:])
+                else:
+                    nc.scalar.copy(out=bias_bc[:, c * 512:(c + 1) * 512], in_=st[:])
+
+        def flip_bank(views, words, eng, ndummy=0):
+            st = stp.tile([P, 512], F32, tag="st")
+            for i in range(ndummy):
+                dummy(st)
             for s in range(4):
                 nc.tensor.transpose(st[:, s * P:(s + 1) * P], views[s], ident[:])
             src = st[:].rearrange("p (j u n) -> p j n u", j=2, u=2)
@@ -136,14 +158,14 @@ def tile_linearmoloralayer_pa_kernel(tc, x, gate_logits, W_base, b_base, A, B, o
             else:
                 nc.scalar.copy(out=dst, in_=src)
 
-        def t_xa(kind, t):
+        def t_xa(kind, t, nd=(0, 0)):
             grp = grpp.tile([P, 2048], BF16, tag="grp", align_bytes=64)
             grps[(kind, t)] = grp
             w = raws[("xa", t)][:].bitcast(F32)
             base = 0 if kind == "x" else 1024
             words = grp[:].bitcast(F32)
             for b in range(2):
-                flip_bank([w[:, base + (4 * b + s) * P:base + (4 * b + s + 1) * P] for s in range(4)], words[:, 512 * b:512 * (b + 1)], "s")
+                flip_bank([w[:, base + (4 * b + s) * P:base + (4 * b + s + 1) * P] for s in range(4)], words[:, 512 * b:512 * (b + 1)], "s", nd[b])
 
         def q_xa(kind, t):
             codes, scales = (xc, xs) if kind == "x" else (ac, asc)
@@ -315,9 +337,11 @@ def tile_linearmoloralayer_pa_kernel(tc, x, gate_logits, W_base, b_base, A, B, o
             arr.append(("x", t))
         done = []
         new_acc("h")
+        warm_up(4)
+        bias_job()
         for k in range(len(arr) + 2):
             if k < len(arr):
-                t_xa(arr[k][0], arr[k][1])
+                t_xa(arr[k][0], arr[k][1], (1, 0) if k < 5 else (0, 0))
             if k == 2:
                 softmax_head()
             if k == 4:

@@ -35,7 +35,7 @@ def tile_linearmoloralayer_pa_kernel(tc, x, gate_logits, W_base, b_base, A, B, o
         const = ctx.enter_context(tc.tile_pool(name="const", bufs=1))
         rawp = ctx.enter_context(tc.tile_pool(name="rawp", bufs=8))
         grpp = ctx.enter_context(tc.tile_pool(name="grpp", bufs=3))
-        bsp = ctx.enter_context(tc.tile_pool(name="bsp", bufs=4))
+        bsp = ctx.enter_context(tc.tile_pool(name="bsp", bufs=6))
         wcp = ctx.enter_context(tc.tile_pool(name="wcp", bufs=3))
         outp = ctx.enter_context(tc.tile_pool(name="outp", bufs=4))
         accp = ctx.enter_context(tc.psum_pool(name="accp", bufs=1))
@@ -52,11 +52,11 @@ def tile_linearmoloralayer_pa_kernel(tc, x, gate_logits, W_base, b_base, A, B, o
         nc.vector.memset(brow[:], 0.0)
         warm = const.tile([P, 1], F32)
         nc.vector.memset(warm[:], 0.0)
+        nc.scalar.dma_start(out=brow[0:1, :], in_=b_base.rearrange("(o n) -> o n", o=1))
         nc.scalar.activation(out=warm[:], in_=warm[:], func=ACT.Exp)
 
         raws = {}
         gl = const.tile([P, TT, E], BF16)
-        nc.sync.dma_start(out=brow[0:1, :], in_=b_base.rearrange("(o n) -> o n", o=1))
         for t in range(TT):
             r = rawp.tile([P, 4096], BF16, tag="raw")
             nc.sync.dma_start(out=r[:, D:2 * D], in_=af[t // 2, t % 2, :, :])
@@ -232,14 +232,16 @@ def tile_linearmoloralayer_pa_kernel(tc, x, gate_logits, W_base, b_base, A, B, o
         def hw_quant():
             nc.vector.quantize_mx(out=hc[:].bitcast(FP8X4), scales=hsc[:], in_=hwg[:])
 
-        def shuffle_b(q):
-            bs = bsp.tile([P, 2048], BF16, tag="bs")
-            grps[("bs", q)] = bs
-            for h in range(2):
-                nc.vector.tensor_copy(
-                    out=bs[:].rearrange("p (s e r) -> p s e r", s=4, r=R)[:, :, 16 * h:16 * h + 16, :],
-                    in_=raws[("b", h)][:].rearrange("p (e s r) -> p s e r", e=16, r=R)[:, 4 * q:4 * q + 4, :, :],
-                )
+        def shuffle_b(q, h, eng="v"):
+            if h == 0:
+                bs = bsp.tile([P, 2048], BF16, tag="bs")
+                grps[("bs", q)] = bs
+            dst = grps[("bs", q)][:].bitcast(F32).rearrange("p (s e r) -> p s e r", s=4, r=R // 2)[:, :, 16 * h:16 * h + 16, :]
+            src = raws[("b", h)][:].bitcast(F32).rearrange("p (e s r) -> p s e r", e=16, r=R // 2)[:, 4 * q:4 * q + 4, :, :]
+            if eng == "v":
+                nc.vector.tensor_copy(out=dst, in_=src)
+            else:
+                nc.scalar.copy(out=dst, in_=src)
 
         def t_b(half, engs):
             bgw = bg[:].bitcast(F32).rearrange("p (n s u) -> p n s u", s=16, u=2)
@@ -337,7 +339,7 @@ def tile_linearmoloralayer_pa_kernel(tc, x, gate_logits, W_base, b_base, A, B, o
             arr.append(("x", t))
         done = []
         new_acc("h")
-        warm_up(4)
+        warm_up(5)
         bias_job()
         for k in range(len(arr) + 2):
             if k < len(arr):
@@ -373,6 +375,8 @@ def tile_linearmoloralayer_pa_kernel(tc, x, gate_logits, W_base, b_base, A, B, o
         p4(0, 0)
         p4(0, 1)
         q_w(0, 1)
+        for q in range(4):
+            shuffle_b(q, 0, "v")
         t_w(1, 0)
         load_w(3, 0)
         p_close(0, (2, 3), (0, 1))
@@ -380,13 +384,13 @@ def tile_linearmoloralayer_pa_kernel(tc, x, gate_logits, W_base, b_base, A, B, o
         p_close(0, (2, 3), (2, 3))
         t_w(1, 1)
         load_w(3, 1)
-        for q in range(2):
-            shuffle_b(q)
+        shuffle_b(0, 1, "v")
+        shuffle_b(1, 1, "v")
         p4(1, 0)
         q_w(1, 1)
         t_b(0, "ss")
-        for q in range(2, 4):
-            shuffle_b(q)
+        shuffle_b(2, 1, "v")
+        shuffle_b(3, 1, "v")
         p4(1, 1)
         t_b(1, "sv")
         p4(1, 2)

@@ -7,6 +7,7 @@ F32 = mybir.dt.float32
 BF16 = mybir.dt.bfloat16
 U32 = mybir.dt.uint32
 U8 = mybir.dt.uint8
+I32 = mybir.dt.int32
 FP8X4 = mybir.dt.float8_e4m3fn_x4
 ALU = mybir.AluOpType
 ACT = mybir.ActivationFunctionType
@@ -44,12 +45,12 @@ def tile_linearmoloralayer_pa_kernel(tc, x, gate_logits, W_base, b_base, A, B, o
 
         ident = const.tile([P, P], F32)
         make_identity(nc, ident[:])
+        zeros = const.tile([P, 512], BF16)
+        nc.vector.memset(zeros[:].bitcast(I32), 0)
         ones = const.tile([P, P], BF16)
         nc.vector.memset(ones[:], 1.0)
-        zeros = const.tile([P, 512], BF16)
-        nc.vector.memset(zeros[:], 0.0)
         brow = bsp.tile([P, O], BF16, tag="bs")
-        nc.vector.memset(brow[:], 0.0)
+        nc.vector.memset(brow[:].bitcast(I32), 0)
         warm = const.tile([P, 1], F32)
         nc.vector.memset(warm[:], 0.0)
         nc.scalar.dma_start(out=brow[0:1, :], in_=b_base.rearrange("(o n) -> o n", o=1))
@@ -136,8 +137,8 @@ def tile_linearmoloralayer_pa_kernel(tc, x, gate_logits, W_base, b_base, A, B, o
             for i in range(n):
                 dummy(st)
 
-        def bias_job():
-            for c in range(NC):
+        def bias_job(cs):
+            for c in cs:
                 st = stp.tile([P, 512], F32, tag="st")
                 nc.tensor.matmul(out=st[:], lhsT=ones[:], rhs=brow[:, c * 512:(c + 1) * 512], start=True, stop=True)
                 if c % 2 == 0:
@@ -339,11 +340,12 @@ def tile_linearmoloralayer_pa_kernel(tc, x, gate_logits, W_base, b_base, A, B, o
             arr.append(("x", t))
         done = []
         new_acc("h")
-        warm_up(5)
-        bias_job()
+        warm_up(9)
         for k in range(len(arr) + 2):
             if k < len(arr):
-                t_xa(arr[k][0], arr[k][1], (1, 0) if k < 5 else (0, 0))
+                if k in (1, 2, 3, 4):
+                    bias_job(((1, 2, 3, 4).index(k),))
+                t_xa(arr[k][0], arr[k][1], (1, 1) if k < 1 else ((0, 1) if k in (1, 2, 3, 5) else (0, 0)))
             if k == 2:
                 softmax_head()
             if k == 4:

@@ -45,15 +45,15 @@ def tile_linearmoloralayer_pa_kernel(tc, x, gate_logits, W_base, b_base, A, B, o
 
         ident = const.tile([P, P], F32)
         make_identity(nc, ident[:])
+        brow = bsp.tile([P, O], BF16, tag="bs")
+        nc.vector.memset(brow[:].bitcast(I32), 0)
+        nc.sync.dma_start(out=brow[0:1, :], in_=b_base.rearrange("(o n) -> o n", o=1))
         zeros = const.tile([P, 512], BF16)
         nc.vector.memset(zeros[:].bitcast(I32), 0)
         ones = const.tile([P, P], BF16)
         nc.vector.memset(ones[:], 1.0)
-        brow = bsp.tile([P, O], BF16, tag="bs")
-        nc.vector.memset(brow[:].bitcast(I32), 0)
         warm = const.tile([P, 1], F32)
         nc.vector.memset(warm[:], 0.0)
-        nc.scalar.dma_start(out=brow[0:1, :], in_=b_base.rearrange("(o n) -> o n", o=1))
         nc.scalar.activation(out=warm[:], in_=warm[:], func=ACT.Exp)
 
         raws = {}
@@ -320,6 +320,44 @@ def tile_linearmoloralayer_pa_kernel(tc, x, gate_logits, W_base, b_base, A, B, o
                     lora_pass(accs[c][tt], c, tt, False, True)
                 evac(c, tt)
 
+        def p4_some(c, g, tts):
+            if g == 0:
+                new_acc(c)
+            for tt in tts:
+                base_pass(c, g, tt, g == 0, False)
+
+        def last_tile_in_halves(c, tt):
+            for half in range(2):
+                if half == 0:
+                    bank = accs[c][tt]
+                else:
+                    bank = stp.tile([P, 512], F32, tag="st", name="lasthalf")
+                cols = slice(c * 512 + half * 256, c * 512 + (half + 1) * 256)
+                for g in range(NG):
+                    wc, ws = wcs[(c, g // 2)]
+                    wcols = slice((g % 2) * 512 + half * 256, (g % 2) * 512 + (half + 1) * 256)
+                    nc.tensor.matmul_mx(
+                        out=bank[:, 0:256],
+                        lhsT=xc[:, tt, g * P:(g + 1) * P].bitcast(FP8X4),
+                        lhsT_scale=xs[:, tt, g * P:(g + 1) * P],
+                        rhs=wc[:, wcols].bitcast(FP8X4),
+                        rhs_scale=ws[:, wcols],
+                        start=(g == 0),
+                        stop=False,
+                    )
+                nc.tensor.matmul_mx(
+                    out=bank[:, 0:256],
+                    lhsT=hc[:, tt * P:(tt + 1) * P].bitcast(FP8X4),
+                    lhsT_scale=hsc[:, tt * P:(tt + 1) * P],
+                    rhs=bc[:, cols].bitcast(FP8X4),
+                    rhs_scale=bsc[:, cols],
+                    start=False,
+                    stop=True,
+                )
+                osb = outp.tile([P, 256], F32, tag="osb")
+                nc.vector.tensor_tensor(out=osb[:], in0=bank[:, 0:256], in1=bias_bc[:, cols], op=ALU.add)
+                nc.sync.dma_start(out=of[tt * P:(tt + 1) * P, cols], in_=osb[:])
+
         def late_lora(c, where):
             banks = []
             for tt in range(TT):
@@ -340,12 +378,11 @@ def tile_linearmoloralayer_pa_kernel(tc, x, gate_logits, W_base, b_base, A, B, o
             arr.append(("x", t))
         done = []
         new_acc("h")
-        warm_up(9)
+        warm_up(5)
+        bias_job((0, 1, 2, 3))
         for k in range(len(arr) + 2):
             if k < len(arr):
-                if k in (1, 2, 3, 4):
-                    bias_job(((1, 2, 3, 4).index(k),))
-                t_xa(arr[k][0], arr[k][1], (1, 1) if k < 1 else ((0, 1) if k in (1, 2, 3, 5) else (0, 0)))
+                t_xa(arr[k][0], arr[k][1], (1, 0) if k < 5 else (0, 0))
             if k == 2:
                 softmax_head()
             if k == 4:

@@ -41,7 +41,6 @@ def tile_linearmoloralayer_pa_kernel(tc, x, gate_logits, W_base, b_base, A, B, o
         outp = ctx.enter_context(tc.tile_pool(name="outp", bufs=4))
         accp = ctx.enter_context(tc.psum_pool(name="accp", bufs=1))
         stp = ctx.enter_context(tc.psum_pool(name="stp", bufs=4))
-        ctx.enter_context(tc.manual_schedule())
 
         ident = const.tile([P, P], F32)
         make_identity(nc, ident[:])

from contextlib import ExitStack

import concourse.mybir as mybir
from concourse.masks import make_identity

F32 = mybir.dt.float32
BF16 = mybir.dt.bfloat16
U32 = mybir.dt.uint32
U8 = mybir.dt.uint8
I32 = mybir.dt.int32
FP8X4 = mybir.dt.float8_e4m3fn_x4
ALU = mybir.AluOpType
ACT = mybir.ActivationFunctionType
AX = mybir.AxisListType

P = 128
TT = 4
D = 2048
O = 2048
E = 32
R = 16
NG = 4
NC = 4
FLOPS = 2 * 512 * D * O + 2 * 512 * D * 512 + 2 * 512 * 512 * O
DEFERRED = (0,)


def tile_linearmoloralayer_pa_kernel(tc, x, gate_logits, W_base, b_base, A, B, out):
    nc = tc.nc
    xf = x.flatten_outer_dims()
    gf = gate_logits.flatten_outer_dims()
    af = A.flatten_outer_dims().rearrange("(u p e) d -> u e p d", u=2, e=2)
    of = out.flatten_outer_dims()

    with ExitStack() as ctx:
        const = ctx.enter_context(tc.tile_pool(name="const", bufs=1))
        rawp = ctx.enter_context(tc.tile_pool(name="rawp", bufs=8))
        grpp = ctx.enter_context(tc.tile_pool(name="grpp", bufs=3))
        bsp = ctx.enter_context(tc.tile_pool(name="bsp", bufs=6))
        wcp = ctx.enter_context(tc.tile_pool(name="wcp", bufs=3))
        outp = ctx.enter_context(tc.tile_pool(name="outp", bufs=4))
        accp = ctx.enter_context(tc.psum_pool(name="accp", bufs=1))
        stp = ctx.enter_context(tc.psum_pool(name="stp", bufs=4))

        ident = const.tile([P, P], F32)
        make_identity(nc, ident[:])
        brow = bsp.tile([P, O], BF16, tag="bs")
        nc.vector.memset(brow[:].bitcast(I32), 0)
        nc.sync.dma_start(out=brow[0:1, :], in_=b_base.rearrange("(o n) -> o n", o=1))
        zeros = const.tile([P, 512], BF16)
        nc.vector.memset(zeros[:].bitcast(I32), 0)
        ones = const.tile([P, P], BF16)
        nc.vector.memset(ones[:], 1.0)
        warm = const.tile([P, 1], F32)
        nc.vector.memset(warm[:], 0.0)
        nc.scalar.activation(out=warm[:], in_=warm[:], func=ACT.Exp)

        raws = {}
        gl = const.tile([P, TT, E], BF16)
        for t in range(TT):
            r = rawp.tile([P, 4096], BF16, tag="raw")
            nc.sync.dma_start(out=r[:, D:2 * D], in_=af[t // 2, t % 2, :, :])
            nc.sync.dma_start(out=r[:, 0:D], in_=xf[t * P:(t + 1) * P, :])
            raws[("xa", t)] = r
            if t == 0:
                nc.sync.dma_start(out=gl[:], in_=gf.rearrange("(t p) e -> p t e", p=P))
        bview = B.rearrange("e (p s) r -> p e (s r)", s=16)

        def load_w(c, d):
            r = rawp.tile([P, 4096], BF16, tag="raw")
            nc.sync.dma_start(
                out=r[:].rearrange("p (j k) -> p j k", j=4),
                in_=W_base[c * 512:(c + 1) * 512, d * 1024:(d + 1) * 1024].rearrange("(j p) k -> p j k", p=P),
            )
            raws[("w", c, d)] = r

        bias_bc = const.tile([P, O], F32)

        def load_b(h):
            r = rawp.tile([P, 4096], BF16, tag="raw")
            nc.sync.dma_start(out=r[:].rearrange("p (e k) -> p e k", e=16), in_=bview[:, 16 * h:16 * h + 16, :])
            raws[("b", h)] = r

        load_w(0, 0)
        load_w(0, 1)
        load_w(1, 0)
        load_b(0)

        xc = const.tile([P, TT, 512], U32, align_bytes=64)
        xs = const.tile([P, TT, 512], U8, align_bytes=64)
        ac = const.tile([P, 4, 512], U32, align_bytes=64)
        asc = const.tile([P, 4, 512], U8, align_bytes=64)
        bc = const.tile([P, O], U32, align_bytes=64)
        bsc = const.tile([P, O], U8, align_bytes=64)
        hc = const.tile([P, 512], U32, align_bytes=64)
        hsc = const.tile([P, 512], U8, align_bytes=64)
        hwg = const.tile([P, 2048], BF16, align_bytes=64)
        bg = const.tile([P, 4 * O], BF16, align_bytes=64)
        rt = const.tile([P, TT, 2, P], F32)
        keep = const.tile([P, len(DEFERRED) * TT, 512], F32)

        rexp = bsp.tile([P, TT, E, 8], F32, tag="bs")

        ex = const.tile([P, TT, E], F32)

        def softmax_head():
            mx = const.tile([P, TT], F32)
            nc.vector.tensor_reduce(out=mx[:], in_=gl[:], axis=AX.X, op=ALU.max)
            dl = const.tile([P, TT, E], F32)
            nc.vector.tensor_tensor(out=dl[:], in0=gl[:], in1=mx[:].unsqueeze(2).to_broadcast([P, TT, E]), op=ALU.subtract)
            nc.scalar.activation(out=ex[:], in_=dl[:], func=ACT.Exp)

        def softmax_tail():
            sm = const.tile([P, TT], F32)
            nc.vector.tensor_reduce(out=sm[:], in_=ex[:], axis=AX.X, op=ALU.add)
            rc = const.tile([P, TT], F32)
            nc.vector.reciprocal(out=rc[:], in_=sm[:])
            rc2 = const.tile([P, TT], F32)
            nc.vector.tensor_scalar_mul(out=rc2[:], in0=rc[:], scalar1=2.0)
            nc.vector.tensor_tensor(
                out=rexp[:],
                in0=ex[:].unsqueeze(3).to_broadcast([P, TT, E, 8]),
                in1=rc2[:].unsqueeze(2).unsqueeze(3).to_broadcast([P, TT, E, 8]),
                op=ALU.mult,
            )

        grps = {}
        wcs = {}
        accs = {}

        def dummy(st):
            nc.tensor.matmul(out=st[:], lhsT=ones[:], rhs=zeros[:], start=True, stop=True)

        def warm_up(n):
            st = stp.tile([P, 512], F32, tag="st")
            for i in range(n):
                dummy(st)

        def bias_job(cs):
            for c in cs:
                st = stp.tile([P, 512], F32, tag="st")
                nc.tensor.matmul(out=st[:], lhsT=ones[:], rhs=brow[:, c * 512:(c + 1) * 512], start=True, stop=True)
                if c % 2 == 0:
                    nc.vector.tensor_copy(out=bias_bc[:, c * 512:(c + 1) * 512], in_=st[:])
                else:
                    nc.scalar.copy(out=bias_bc[:, c * 512:(c + 1) * 512], in_=st[:])

        def flip_bank(views, words, eng, ndummy=0):
            st = stp.tile([P, 512], F32, tag="st")
            for i in range(ndummy):
                dummy(st)
            for s in range(4):
                nc.tensor.transpose(st[:, s * P:(s + 1) * P], views[s], ident[:])
            src = st[:].rearrange("p (j u n) -> p j n u", j=2, u=2)
            dst = words.rearrange("p (j n u) -> p j n u", j=2, u=2)
            if eng == "v":
                nc.vector.tensor_copy(out=dst, in_=src)
            else:
                nc.scalar.copy(out=dst, in_=src)

        def t_xa(kind, t, nd=(0, 0)):
            grp = grpp.tile([P, 2048], BF16, tag="grp", align_bytes=64)
            grps[(kind, t)] = grp
            w = raws[("xa", t)][:].bitcast(F32)
            base = 0 if kind == "x" else 1024
            words = grp[:].bitcast(F32)
            for b in range(2):
                flip_bank([w[:, base + (4 * b + s) * P:base + (4 * b + s + 1) * P] for s in range(4)], words[:, 512 * b:512 * (b + 1)], "s", nd[b])

        def q_xa(kind, t):
            codes, scales = (xc, xs) if kind == "x" else (ac, asc)
            nc.vector.quantize_mx(out=codes[:, t, :].bitcast(FP8X4), scales=scales[:, t, :], in_=grps[(kind, t)][:])

        def t_w(c, d, engs="ssss"):
            grp = grpp.tile([P, 4096], BF16, tag="grp", align_bytes=64)
            grps[("w", c, d)] = grp
            w = raws[("w", c, d)][:].bitcast(F32)
            words = grp[:].bitcast(F32)
            for k in range(2):
                for b in range(2):
                    views = [w[:, (2 * b + s // 2) * 512 + k * 256 + (s % 2) * P:(2 * b + s // 2) * 512 + k * 256 + (s % 2) * P + P] for s in range(4)]
                    flip_bank(views, words[:, 1024 * k + 512 * b:1024 * k + 512 * (b + 1)], engs[2 * k + b])

        def q_w(c, d):
            wc = wcp.tile([P, 1024], U32, tag="wc", align_bytes=64)
            ws = wcp.tile([P, 1024], U8, tag="ws", align_bytes=64)
            wcs[(c, d)] = (wc, ws)
            for k in range(2):
                nc.vector.quantize_mx(
                    out=wc[:, k * 512:(k + 1) * 512].bitcast(FP8X4),
                    scales=ws[:, k * 512:(k + 1) * 512],
                    in_=grps[("w", c, d)][:, k * 2048:(k + 1) * 2048],
                )

        def new_acc(key):
            tiles = []
            for tt in range(TT):
                a = accp.tile([P, 512], F32, tag="acc%d" % tt, name="acc%d" % tt)
                tiles.append(a)
            accs[key] = tiles
            return tiles

        def route_job():
            rw = rexp[:].rearrange("p t e i -> p t (e i)")
            for b in range(2):
                st = stp.tile([P, 512], F32, tag="st")
                for s in range(4):
                    nc.tensor.transpose(st[:, s * P:(s + 1) * P], rw[:, 2 * b + s // 2, (s % 2) * P:(s % 2 + 1) * P], ident[:])
                nc.scalar.copy(out=rt[:, 2 * b:2 * b + 2, :, :].rearrange("p t u n -> p (t u n)"), in_=st[:])

        def h_group(t, tt):
            hps = accs["h"]
            for g in range(NG):
                nc.tensor.matmul_mx(
                    out=hps[tt][:, t * P:(t + 1) * P],
                    lhsT=ac[:, t, g * P:(g + 1) * P].bitcast(FP8X4),
                    lhsT_scale=asc[:, t, g * P:(g + 1) * P],
                    rhs=xc[:, tt, g * P:(g + 1) * P].bitcast(FP8X4),
                    rhs_scale=xs[:, tt, g * P:(g + 1) * P],
                    start=(g == 0),
                    stop=(g == NG - 1),
                )

        def hw_mult(tt):
            nc.vector.tensor_tensor(
                out=hwg[:, tt * 512:(tt + 1) * 512].rearrange("p (n u e) -> p n u e", u=2, e=2),
                in0=accs["h"][tt][:].rearrange("p (u e n) -> p n u e", u=2, e=2),
                in1=rt[:, tt, :, :].rearrange("p u n -> p n u").unsqueeze(3).to_broadcast([P, P, 2, 2]),
                op=ALU.mult,
            )

        def hw_quant():
            nc.vector.quantize_mx(out=hc[:].bitcast(FP8X4), scales=hsc[:], in_=hwg[:])

        def shuffle_b(q, h, eng="v"):
            if h == 0:
                bs = bsp.tile([P, 2048], BF16, tag="bs")
                grps[("bs", q)] = bs
            dst = grps[("bs", q)][:].bitcast(F32).rearrange("p (s e r) -> p s e r", s=4, r=R // 2)[:, :, 16 * h:16 * h + 16, :]
            src = raws[("b", h)][:].bitcast(F32).rearrange("p (e s r) -> p s e r", e=16, r=R // 2)[:, 4 * q:4 * q + 4, :, :]
            if eng == "v":
                nc.vector.tensor_copy(out=dst, in_=src)
            else:
                nc.scalar.copy(out=dst, in_=src)

        def t_b(half, engs):
            bgw = bg[:].bitcast(F32).rearrange("p (n s u) -> p n s u", s=16, u=2)
            for q in (2 * half, 2 * half + 1):
                bw = grps[("bs", q)][:].bitcast(F32)
                for b in range(2):
                    st = stp.tile([P, 512], F32, tag="st")
                    for s in range(4):
                        col = (2 * b + s // 2) * 256 + (s % 2) * P
                        nc.tensor.transpose(st[:, s * P:(s + 1) * P], bw[:, col:col + P], ident[:])
                    os0 = 4 * q + 2 * b
                    src = st[:].rearrange("p (s u n) -> p n s u", s=2, u=2)
                    if engs[q % 2] == "v":
                        nc.vector.tensor_copy(out=bgw[:, :, os0:os0 + 2, :], in_=src)
                    else:
                        nc.scalar.copy(out=bgw[:, :, os0:os0 + 2, :], in_=src)

        def q_b(hs):
            for h in hs:
                nc.vector.quantize_mx(
                    out=bc[:, h * 1024:(h + 1) * 1024].bitcast(FP8X4),
                    scales=bsc[:, h * 1024:(h + 1) * 1024],
                    in_=bg[:, h * 4096:(h + 1) * 4096],
                )

        def lora_pass(dst, c, tt, start, stop):
            nc.tensor.matmul_mx(
                out=dst[:],
                lhsT=hc[:, tt * P:(tt + 1) * P].bitcast(FP8X4),
                lhsT_scale=hsc[:, tt * P:(tt + 1) * P],
                rhs=bc[:, c * 512:(c + 1) * 512].bitcast(FP8X4),
                rhs_scale=bsc[:, c * 512:(c + 1) * 512],
                start=start,
                stop=stop,
            )

        def base_pass(c, g, tt, start, stop):
            wc, ws = wcs[(c, g // 2)]
            k = g % 2
            nc.tensor.matmul_mx(
                out=accs[c][tt][:],
                lhsT=xc[:, tt, g * P:(g + 1) * P].bitcast(FP8X4),
                lhsT_scale=xs[:, tt, g * P:(g + 1) * P],
                rhs=wc[:, k * 512:(k + 1) * 512].bitcast(FP8X4),
                rhs_scale=ws[:, k * 512:(k + 1) * 512],
                start=start,
                stop=stop,
            )

        def store(c, tt, src):
            nc.sync.dma_start(out=of[tt * P:(tt + 1) * P, c * 512:(c + 1) * 512], in_=src)

        def p4(c, g):
            if g == 0:
                new_acc(c)
            for tt in range(TT):
                base_pass(c, g, tt, g == 0, False)

        def evac(c, tt):
            if c in DEFERRED:
                dst = keep[:, DEFERRED.index(c) * TT + tt, :]
            else:
                osb = outp.tile([P, 512], F32, tag="osb")
                dst = osb[:]
            nc.vector.tensor_tensor(out=dst, in0=accs[c][tt][:], in1=bias_bc[:, c * 512:(c + 1) * 512], op=ALU.add)
            if c not in DEFERRED:
                store(c, tt, dst)

        def p_close(c, gs, tts):
            late = c in DEFERRED
            for tt in tts:
                for g in gs:
                    base_pass(c, g, tt, False, late and g == NG - 1)
                if not late:
                    lora_pass(accs[c][tt], c, tt, False, True)
                evac(c, tt)

        def p4_some(c, g, tts):
            if g == 0:
                new_acc(c)
            for tt in tts:
                base_pass(c, g, tt, g == 0, False)

        def last_tile_in_halves(c, tt):
            for half in range(2):
                if half == 0:
                    bank = accs[c][tt]
                else:
                    bank = stp.tile([P, 512], F32, tag="st", name="lasthalf")
                cols = slice(c * 512 + half * 256, c * 512 + (half + 1) * 256)
                for g in range(NG):
                    wc, ws = wcs[(c, g // 2)]
                    wcols = slice((g % 2) * 512 + half * 256, (g % 2) * 512 + (half + 1) * 256)
                    nc.tensor.matmul_mx(
                        out=bank[:, 0:256],
                        lhsT=xc[:, tt, g * P:(g + 1) * P].bitcast(FP8X4),
                        lhsT_scale=xs[:, tt, g * P:(g + 1) * P],
                        rhs=wc[:, wcols].bitcast(FP8X4),
                        rhs_scale=ws[:, wcols],
                        start=(g == 0),
                        stop=False,
                    )
                nc.tensor.matmul_mx(
                    out=bank[:, 0:256],
                    lhsT=hc[:, tt * P:(tt + 1) * P].bitcast(FP8X4),
                    lhsT_scale=hsc[:, tt * P:(tt + 1) * P],
                    rhs=bc[:, cols].bitcast(FP8X4),
                    rhs_scale=bsc[:, cols],
                    start=False,
                    stop=True,
                )
                osb = outp.tile([P, 256], F32, tag="osb")
                nc.vector.tensor_tensor(out=osb[:], in0=bank[:, 0:256], in1=bias_bc[:, cols], op=ALU.add)
                nc.sync.dma_start(out=of[tt * P:(tt + 1) * P, cols], in_=osb[:])

        def late_lora(c, where):
            banks = []
            for tt in range(TT):
                if where == "acc":
                    a = accp.tile([P, 512], F32, tag="acc%d" % tt, name="late%d" % tt)
                else:
                    a = stp.tile([P, 512], F32, tag="st", name="late")
                banks.append(a)
                lora_pass(a, c, tt, True, True)
            for tt in range(TT):
                osb = outp.tile([P, 512], F32, tag="osb")
                nc.vector.tensor_tensor(out=osb[:], in0=banks[tt][:], in1=keep[:, DEFERRED.index(c) * TT + tt, :], op=ALU.add)
                store(c, tt, osb[:])

        arr = []
        for t in range(TT):
            arr.append(("a", t))
            arr.append(("x", t))
        done = []
        new_acc("h")
        warm_up(5)
        bias_job((0, 1, 2, 3))
        for k in range(len(arr) + 2):
            if k < len(arr):
                t_xa(arr[k][0], arr[k][1], (1, 0) if k < 5 else (0, 0))
            if k == 2:
                softmax_head()
            if k == 4:
                softmax_tail()
            if k == 5:
                route_job()
            if k == 8:
                load_w(1, 1)
                load_b(1)
                load_w(2, 0)
                load_w(2, 1)
                t_w(0, 0)
            if 1 <= k <= len(arr):
                q_xa(arr[k - 1][0], arr[k - 1][1])
            if k == 9:
                q_w(0, 0)
                t_w(0, 1)
            if 2 <= k:
                done.append(arr[k - 2])
                for t2 in range(TT):
                    for t1 in range(4):
                        if ("a", t1) in done and ("x", t2) in done and (t1, t2) not in done:
                            done.append((t1, t2))
                            h_group(t1, t2)
                            if t1 == 3:
                                hw_mult(t2)

        hw_quant()
        p4(0, 0)
        p4(0, 1)
        q_w(0, 1)
        for q in range(4):
            shuffle_b(q, 0, "v")
        t_w(1, 0)
        load_w(3, 0)
        p_close(0, (2, 3), (0, 1))
        q_w(1, 0)
        p_close(0, (2, 3), (2, 3))
        t_w(1, 1)
        load_w(3, 1)
        shuffle_b(0, 1, "v")
        shuffle_b(1, 1, "v")
        p4(1, 0)
        q_w(1, 1)
        t_b(0, "ss")
        shuffle_b(2, 1, "v")
        shuffle_b(3, 1, "v")
        p4(1, 1)
        t_b(1, "sv")
        p4(1, 2)
        t_w(2, 0)
        q_b((0,))
        p4(1, 3)
        q_w(2, 0)
        p_close(1, (), (0, 1, 2, 3))
        t_w(2, 1)
        late_lora(0, "acc")
        q_w(2, 1)
        t_w(3, 0)
        q_b((1,))
        p4(2, 0)
        p4(2, 1)
        q_w(3, 0)
        t_w(3, 1)
        p_close(2, (2, 3), (0, 1, 2, 3))
        q_w(3, 1)
        p4(3, 0)
        p4(3, 1)
        p_close(3, (2, 3), (0, 1, 2, 3))
